import numpy as np
import ml_dtypes


def mxq(x, axis, fmt="e4m3"):
    dtype, down = {"e4m3": (ml_dtypes.float8_e4m3fn, 7), "e5m2": (ml_dtypes.float8_e5m2, 14)}[fmt]
    v = np.moveaxis(np.asarray(x, np.float32).astype(ml_dtypes.bfloat16).astype(np.float64), axis, -1)
    blocks = v.reshape(v.shape[:-1] + (-1, 32))
    amax = np.abs(blocks).max(-1, keepdims=True)
    byte = np.maximum(np.where(amax > 0, np.frexp(amax)[1] - 1 + 127, 0) - down, 1)
    scale = np.exp2(byte - 127.0)
    codes = (blocks / scale).astype(np.float32).astype(dtype).astype(np.float64)
    return np.moveaxis((codes * scale).reshape(v.shape), -1, axis)


WIDE = False


def mx_kscale(k):
    if not WIDE:
        return np.ones(k)
    levels = np.array([10, -10, 5, -5, 0])
    if k % 512:
        return np.exp2(np.random.permutation(np.resize(levels, k // 32))).repeat(32)
    a = np.empty((k // 512, 16))
    for p in range(k // 512):
        a[p, :8] = np.random.permutation(np.resize(levels, 8))
        for g in range(8):
            far = levels[np.abs(levels - a[p, g]) >= 10]
            a[p, g + 8] = far[np.random.randint(len(far))]
    return np.exp2(a.ravel()).repeat(32)


BF16 = ml_dtypes.bfloat16


def bf(x):
    return np.asarray(x, np.float32).astype(BF16)


def f64(x):
    return np.asarray(x).astype(np.float64)


B, S, I0, I1, I2, I3, I4, O0, O1, O2, O3, O4, R1, R2, R3, R4 = 2, 256, 4, 4, 2, 2, 16, 4, 8, 2, 2, 32, 16, 512, 1024, 512
IA, OA = I0 * I1, O0 * O1


def tt_step(t, c):
    I, O, r = t.shape
    _, i, o, q = c.shape
    p = mxq(t.reshape(I * O, r), 1, "e4m3") @ mxq(c.reshape(r, i * o * q), 0, "e4m3")
    return p.reshape(I, O, i, o, q).transpose(0, 2, 1, 3, 4).reshape(I * i, O * o, q)


def draw0():
    s, u = mx_kscale(R2), mx_kscale(R3)
    return {"t1": bf(np.random.standard_normal((IA, OA, R2)) * s),
            "core2": bf(np.random.standard_normal((R2, I2, O2, R3)) / np.sqrt(R2) / s[:, None, None, None] * u),
            "core3": bf(np.random.standard_normal((R3, I3, O3, R4)) / np.sqrt(R3) / u[:, None, None, None])}


def core(t1, core2, core3):
    t2 = tt_step(f64(t1), f64(core2))
    return tt_step(t2, f64(core3))


def e4m3fn_bytes(y):
    return np.clip(np.asarray(y, np.float64), -448.0, 448.0).astype(np.float32).astype(ml_dtypes.float8_e4m3fn).view(np.uint8)


def e4m3fn_values(b):
    return np.asarray(b, np.uint8).view(ml_dtypes.float8_e4m3fn).astype(np.float64)


def setup_inputs():
    d = draw0()
    x0 = np.asarray(d['core3']).astype(np.float64)
    s = (np.max(np.abs(x0), axis=(1, 2, 3), keepdims=True) / 448.0).astype(np.float32)
    out = {}
    for k, v in d.items():
        if k == 'core3':
            out['core3_bytes'] = e4m3fn_bytes(x0 / s.astype(np.float64))
            out['core3_scale'] = s
        else:
            out[k] = v
    return out


def reference(t1, core2, core3_bytes, core3_scale):
    return core(t1, core2, e4m3fn_values(core3_bytes) * core3_scale.astype(np.float64))

@@ -1,0 +1,237 @@
+from contextlib import ExitStack
+
+import concourse.mybir as mybir
+from concourse.masks import make_identity
+
+F32 = mybir.dt.float32
+BF16 = mybir.dt.bfloat16
+U32 = mybir.dt.uint32
+U8 = mybir.dt.uint8
+FP8 = mybir.dt.float8_e4m3fn
+FP8X4 = mybir.dt.float8_e4m3fn_x4
+MULT = mybir.AluOpType.mult
+COPY = mybir.ActivationFunctionType.Copy
+
+FLOPS = 2 * 512 * 512 * 4096 + 2 * 2048 * 1024 * 2048
+
+
+def deps(o):
+    n, a = o[0], o[1:]
+    if n == "t1c":
+        return [("tr", 2 * a[0]), ("tr", 2 * a[0] + 1)]
+    if n == "t1q":
+        return [("t1c", 0), ("t1c", 1)]
+    if n == "c2q":
+        return [("c2i",) + a]
+    if n == "s1":
+        return [("c2q", a[0], a[1]), ("t1q",)]
+    if n == "ev1":
+        return [("s1",) + a]
+    if n == "t2q":
+        return [("ev1", a[0], a[1], r) for r in range(4)]
+    if n == "c3i":
+        return [("w", a[0], a[1], t) for t in range(4)]
+    if n == "c3q":
+        return [("c3i",) + a]
+    if n == "s2":
+        return [("t2q", a[0], 0), ("t2q", a[0], 1), ("c3q", a[1], 0), ("c3q", a[1], 1)]
+    if n == "ev2":
+        return [("s2",) + a]
+    return []
+
+
+def merge(queues):
+    pos = {"PE": 0, "S": 0, "V": 0}
+    done = set()
+    text = []
+    live = 0
+    while len(text) < len(queues["PE"]) + len(queues["S"]) + len(queues["V"]):
+        before = len(text)
+        for e in ("PE", "S", "V"):
+            while pos[e] < len(queues[e]):
+                o = queues[e][pos[e]]
+                opens = e == "PE" and not (o[0] == "tr" and o[1] % 2 == 1)
+                if opens and live >= 8:
+                    break
+                if not all(d in done for d in deps(o)):
+                    break
+                if opens:
+                    live += 1
+                if o[0] in ("ev1", "ev2", "t1c"):
+                    live -= 1
+                text.append((e,) + o)
+                done.add(o)
+                pos[e] += 1
+        assert len(text) > before
+    return text
+
+
+LOADS = [["t1",0,0],["t1",1,0],["c3",1,0],["c3",1,1],["c2",2,0],["c2",0,0],["c2",1,1],["c2",0,1],["c3",0,0],["c2",2,1],["c2",1,0],["c3",0,1],["c2",3,None]]
+LAST = (3, 0)
+
+
+def parse(text):
+    ops = []
+    for item in text.split(", "):
+        w = item.split(" ")
+        ops.append((w[0],) + tuple(int(x) for x in w[1:]))
+    return ops
+
+
+def queues():
+    return {
+        "PE": parse("tr 0, tr 1, tr 2, tr 3, s1 0 0 0, s1 0 0 1, s1 0 0 2, s1 0 0 3, s1 0 1 0, s1 0 1 1, s1 0 1 2, s1 0 1 3, s1 2 0 0, s1 2 0 1, s1 2 0 2, s1 2 0 3, s1 2 1 0, s1 2 1 1, s1 2 1 2, s1 2 1 3, s1 1 0 0, s1 1 0 1, s1 1 0 2, s1 1 0 3, s1 1 1 0, s1 1 1 1, s1 1 1 2, s1 1 1 3, s2 0 2 0, s2 0 2 1, s2 0 2 2, s2 0 2 3, s2 0 3 0, s2 0 3 1, s2 0 3 2, s2 0 3 3, s2 1 3 0, s2 1 3 1, s2 1 3 2, s2 1 3 3, s2 1 2 0, s2 1 2 1, s2 1 2 2, s2 1 2 3, s2 2 3 0, s2 2 3 1, s2 2 3 2, s2 2 3 3, s2 2 2 0, s2 2 2 1, s2 2 2 2, s2 2 2 3, s2 1 0 0, s2 1 0 1, s2 1 0 2, s2 1 0 3, s2 2 0 0, s2 2 0 1, s2 2 0 2, s2 2 0 3, s2 2 1 0, s2 2 1 1, s2 2 1 2, s2 2 1 3, s2 1 1 0, s2 1 1 1, s2 1 1 2, s2 1 1 3, s2 0 0 0, s2 0 0 1, s2 0 0 2, s2 0 0 3, s1 3 0 0, s1 3 0 1, s1 3 0 2, s1 3 0 3, s1 3 1 0, s1 3 1 1, s1 3 1 2, s1 3 1 3, s2 0 1 0, s2 0 1 1, s2 0 1 2, s2 0 1 3, s2 3 3 0, s2 3 3 1, s2 3 3 2, s2 3 3 3, s2 3 2 0, s2 3 2 1, s2 3 2 2, s2 3 2 3, s2 3 0 0, s2 3 0 1, s2 3 0 2, s2 3 0 3, s2 3 1 0, s2 3 1 1, s2 3 1 2, s2 3 1 3"),
+        "S": parse("t1c 0, t1c 1, w 2 0 1, w 2 0 2, w 2 1 0, w 2 1 2, w 2 1 3, w 3 0 1, w 3 0 2, w 3 0 3, w 3 1 0, w 3 1 1, w 3 1 2, w 3 1 3, w 0 0 0, w 0 0 1, w 0 0 2, w 0 0 3, ev1 0 0 0, ev1 0 0 1, ev1 0 0 2, ev1 0 0 3, ev1 0 1 0, ev1 0 1 1, ev1 0 1 2, ev1 0 1 3, ev1 2 0 0, ev1 2 0 1, ev1 2 0 2, ev1 2 0 3, ev1 2 1 0, ev1 2 1 1, ev1 2 1 2, ev1 2 1 3, w 0 1 0, ev1 1 0 0, ev1 1 0 1, ev1 1 0 2, ev1 1 0 3, ev1 1 1 0, ev1 1 1 1, ev1 1 1 2, ev1 1 1 3, ev2 0 2 0, ev2 0 2 1, ev2 0 2 2, ev2 0 2 3, ev2 0 3 0, ev2 0 3 1, ev2 0 3 3, ev2 1 3 1, ev2 1 3 3, ev2 1 2 0, ev2 1 2 1, ev2 1 2 2, ev2 1 2 3, ev2 2 3 0, ev2 2 3 1, ev2 2 3 2, ev2 2 3 3, ev2 2 2 0, ev2 2 2 1, w 1 1 1, w 1 1 2, w 1 1 3, ev2 1 0 1, ev2 1 0 2, ev2 1 0 3, ev2 2 0 0, ev2 2 0 1, ev2 2 0 2, ev2 2 0 3, ev2 2 1 0, ev2 2 1 1, ev2 2 1 2, ev2 2 1 3, ev2 1 1 0, ev2 1 1 1, ev2 1 1 2, ev2 1 1 3, ev2 0 0 0, ev2 0 0 1, ev2 0 0 2, ev2 0 0 3, ev1 3 0 1, ev1 3 0 3, ev1 3 1 1, ev1 3 1 2, ev2 0 1 0, ev2 0 1 1, ev2 0 1 2, ev2 0 1 3, ev2 3 3 0, ev2 3 3 1, ev2 3 3 2, ev2 3 3 3, ev2 3 2 0, ev2 3 2 1, ev2 3 2 2, ev2 3 2 3, ev2 3 0 0, ev2 3 0 1, ev2 3 0 2, ev2 3 0 3, ev2 3 1 0, ev2 3 1 1, ev2 3 1 2, ev2 3 1 3"),
+        "V": parse("w 2 0 0, t1q, w 2 0 3, w 2 1 1, c3i 2 0, w 3 0 0, c3i 2 1, c3q 2 0, c3q 2 1, c2i 0 0, c2i 0 1, c2q 0 0, c2q 0 1, c2i 2 0, c2i 2 1, c2q 2 0, c2q 2 1, t2q 0 0, t2q 0 1, c2i 1 0, c2i 1 1, c2q 1 0, c2q 1 1, c3i 3 0, c3i 3 1, t2q 1 0, c3q 3 0, c3q 3 1, t2q 2 0, t2q 1 1, t2q 2 1, c3i 0 0, ev2 0 3 2, ev2 1 3 0, ev2 1 3 2, w 0 1 1, w 0 1 2, w 0 1 3, w 1 0 0, c3i 0 1, c3q 0 0, c3q 0 1, w 1 0 1, w 1 0 2, w 1 0 3, w 1 1 0, c3i 1 0, ev2 2 2 2, ev2 2 2 3, ev2 1 0 0, c3i 1 1, c3q 1 0, c3q 1 1, c2i 3 0, c2q 3 0, c2i 3 1, c2q 3 1, ev1 3 0 0, ev1 3 0 2, ev1 3 1 0, t2q 3 0, ev1 3 1 3, t2q 3 1"),
+    }
+
+
+def tile_linear2mpo_pa_kernel(tc, t1, core2, core3_bytes, core3_scale, out):
+    nc = tc.nc
+    with ExitStack() as ctx:
+        keep = ctx.enter_context(tc.tile_pool(name="keep", bufs=1))
+        mid = ctx.enter_context(tc.tile_pool(name="mid", bufs=3))
+        stage = ctx.enter_context(tc.tile_pool(name="stage", bufs=3))
+        psum = ctx.enter_context(tc.psum_pool(name="psum", bufs=8))
+
+        t1_rows = t1.rearrange("i o k -> (i o) k")
+        core2_v = core2.rearrange("(p j) i o q -> p j (i o) q", j=4)
+        core3_v = core3_bytes.rearrange("(g p t) i o q -> g p t (i o q)", g=2, t=4)
+        out_v = out.rearrange("(R s i j) (O o h) q -> s i j o O R (h q)", s=4, i=2, j=2, o=2, h=2)
+
+        ident = keep.tile([128, 128], F32, name="ident")
+        perm = keep.tile([128, 128], F32, name="perm")
+        scale = keep.tile([128, 2, 4], F32, name="scale")
+        t1_raw = keep.tile([128, 4, 512], BF16, name="t1_raw")
+        t1_grouped = keep.tile([128, 512, 4], BF16, name="t1_grouped", align_bytes=64)
+        t1_codes = keep.tile([128, 512], U32, name="t1_codes", align_bytes=64)
+        t1_scales = keep.tile([128, 512], U8, name="t1_scales", align_bytes=64)
+        c2_raw = [keep.tile([128, 4, 1024], BF16, name="c2_raw_%d" % io) for io in range(4)]
+        c3_raw = {}
+        c2_codes, c2_scales, t2_codes, t2_scales, c3_codes, c3_scales = {}, {}, {}, {}, {}, {}
+        for a in range(4):
+            for g in range(2):
+                c2_codes[a, g] = keep.tile([128, 512], U32, name="c2_codes_%d_%d" % (a, g), align_bytes=64)
+                c2_scales[a, g] = keep.tile([128, 512], U8, name="c2_scales_%d_%d" % (a, g), align_bytes=64)
+                t2_codes[a, g] = keep.tile([128, 512], U32, name="t2_codes_%d_%d" % (a, g), align_bytes=64)
+                t2_scales[a, g] = keep.tile([128, 512], U8, name="t2_scales_%d_%d" % (a, g), align_bytes=64)
+                c3_codes[a, g] = keep.tile([128, 512], U32, name="c3_codes_%d_%d" % (a, g), align_bytes=64)
+                c3_scales[a, g] = keep.tile([128, 512], U8, name="c3_scales_%d_%d" % (a, g), align_bytes=64)
+        for h in range(2):
+            for g in range(2):
+                c3_raw[h, g] = keep.tile([128, 4, 1024], U8, name="c3_raw_%d_%d" % (h, g))
+
+        live = {}
+
+        def copy(e, out_ap, in_ap):
+            if e == "S":
+                nc.scalar.copy(out_ap, in_ap)
+            else:
+                nc.vector.tensor_copy(out=out_ap, in_=in_ap)
+
+        def load(kind, a, g):
+            if kind == "t1":
+                nc.sync.dma_start(out=t1_raw[:, 2 * a : 2 * a + 2, :], in_=t1_rows[a * 256 : (a + 1) * 256, :].rearrange("(r p) k -> p r k", r=2))
+            elif kind == "c2" and g is None:
+                nc.sync.dma_start(out=c2_raw[a][:], in_=core2_v[:, :, a, :])
+            elif kind == "c2":
+                cols = slice(g * 512, (g + 1) * 512)
+                nc.sync.dma_start(out=c2_raw[a][:, :, cols], in_=core2_v[:, :, a, cols])
+            else:
+                nc.sync.dma_start(out=c3_raw[a, g][:], in_=core3_v[g][:, :, a * 1024 : (a + 1) * 1024])
+
+        def emit(e, n, *a):
+            if n == "tr":
+                r = a[0]
+                if r % 2 == 0:
+                    live["xt", r // 2] = psum.tile([128, 512], F32, name="bank")
+                xt = live["xt", r // 2][:].rearrange("p (s u n) -> p s u n", s=2, u=2)
+                words = t1_raw[:, r, :].bitcast(F32)
+                for u in range(2):
+                    nc.tensor.transpose(xt[:, r % 2, u, :], words[:, u::2], perm[:])
+            elif n == "t1c":
+                dst = t1_grouped[:, a[0] * 256 : (a[0] + 1) * 256, :].rearrange("p n j -> p (n j)").bitcast(F32)
+                copy(e, dst.rearrange("p (s n u) -> p s n u", s=2, u=2),
+                     live["xt", a[0]][:].rearrange("p (s u n) -> p s n u", s=2, u=2))
+            elif n == "t1q":
+                nc.vector.quantize_mx(out=t1_codes[:].bitcast(FP8X4), scales=t1_scales[:],
+                                      in_=t1_grouped[:].rearrange("p n j -> p (n j)"))
+            elif n == "c2i":
+                io, g = a
+                grouped = mid.tile([128, 512, 4], BF16, name="c2_grouped", align_bytes=64)
+                live["c2g", io, g] = grouped
+                copy(e, grouped[:].rearrange("p (t m) j -> p t m j", t=4),
+                     c2_raw[io][:, :, g * 512 : (g + 1) * 512].rearrange("p j (m t) -> p t m j", t=4))
+            elif n == "c2q":
+                nc.vector.quantize_mx(out=c2_codes[a][:].bitcast(FP8X4), scales=c2_scales[a][:],
+                                      in_=live["c2g", a[0], a[1]][:].rearrange("p n j -> p (n j)"))
+            elif n == "s1":
+                io, g, r = a
+                bank = psum.tile([128, 512], F32, name="bank")
+                live["b1", io, g, r] = bank
+                rows = slice(r * 128, (r + 1) * 128)
+                for t in range(4):
+                    cols = slice(t * 128, (t + 1) * 128)
+                    nc.tensor.matmul_mx(out=bank[:, cols],
+                                        lhsT=c2_codes[io, g][:, cols].bitcast(FP8X4), lhsT_scale=c2_scales[io, g][:, cols],
+                                        rhs=t1_codes[:, rows].bitcast(FP8X4), rhs_scale=t1_scales[:, rows],
+                                        start=True, stop=True)
+            elif n == "ev1":
+                io, g, r = a
+                if ("t2g", io, g) not in live:
+                    live["t2g", io, g] = mid.tile([128, 512, 4], BF16, name="t2_grouped", align_bytes=64)
+                copy(e, live["t2g", io, g][:, r * 128 : (r + 1) * 128, :],
+                     live["b1", io, g, r][:].rearrange("p (t n) -> p n t", t=4))
+            elif n == "t2q":
+                nc.vector.quantize_mx(out=t2_codes[a][:].bitcast(FP8X4), scales=t2_scales[a][:],
+                                      in_=live["t2g", a[0], a[1]][:].rearrange("p n j -> p (n j)"))
+            elif n == "w":
+                c, g, t = a
+                if ("c3w", c, g) not in live:
+                    live["c3w", c, g] = mid.tile([128, 4, 512], BF16, name="c3_wide", align_bytes=64)
+                src = c3_raw[c // 2, g][:, t, (c % 2) * 512 : (c % 2 + 1) * 512].bitcast(FP8)
+                dst = live["c3w", c, g][:, t, :]
+                if e == "S":
+                    nc.scalar.activation(out=dst, in_=src, func=COPY, scale=scale[:, g, t : t + 1])
+                else:
+                    nc.vector.tensor_scalar(out=dst, in0=src, scalar1=scale[:, g, t : t + 1], scalar2=None, op0=MULT)
+            elif n == "c3i":
+                c, g = a
+                live["c3g", c, g] = mid.tile([128, 512, 4], BF16, name="c3_grouped", align_bytes=64)
+                copy(e, live["c3g", c, g][:], live["c3w", c, g][:].rearrange("p t n -> p n t"))
+            elif n == "c3q":
+                nc.vector.quantize_mx(out=c3_codes[a][:].bitcast(FP8X4), scales=c3_scales[a][:],
+                                      in_=live["c3g", a[0], a[1]][:].rearrange("p n j -> p (n j)"))
+            elif n == "s2":
+                io, c, r = a
+                bank = psum.tile([128, 512], F32, name="bank")
+                live["b2", io, c, r] = bank
+                rows = slice(r * 128, (r + 1) * 128)
+                for g in range(2):
+                    nc.tensor.matmul_mx(out=bank[:],
+                                        lhsT=t2_codes[io, g][:, rows].bitcast(FP8X4), lhsT_scale=t2_scales[io, g][:, rows],
+                                        rhs=c3_codes[c, g][:].bitcast(FP8X4), rhs_scale=c3_scales[c, g][:],
+                                        start=(g == 0), stop=(g == 1))
+            elif n == "ev2":
+                io, c, r = a
+                j = c // 2
+                if ("st", io, j) not in live:
+                    live["st", io, j] = stage.tile([128, 4, 1024], F32, name="result")
+                    live["n", io, j] = []
+                result = live["st", io, j]
+                copy(e, result[:, r, (c % 2) * 512 : (c % 2 + 1) * 512], live["b2", io, c, r][:])
+                live["n", io, j].append(r)
+                group = 2 if (io, j) == LAST else 4
+                r0 = r - r % group
+                if len([x for x in live["n", io, j] if r0 <= x < r0 + group]) == 2 * group:
+                    for s in range(4):
+                        nc.sync.dma_start(out=out_v[s, io // 2, j, io % 2][:, r0 : r0 + group, :], in_=result[s:128:4, r0 : r0 + group, :])
+
+        with tc.manual_schedule():
+            make_identity(nc, ident[:])
+            nc.vector.tensor_copy(out=perm[:].rearrange("p (o i) -> p i o", i=4), in_=ident[:].rearrange("p (i o) -> p i o", i=4))
+            nc.scalar.dma_start(out=scale[:], in_=core3_scale.rearrange("(g p t) a b c -> p g (t a b c)", g=2, t=4))
+            for kind, a, g in LOADS:
+                load(kind, a, g)
+            for step in merge(queues()):
+                emit(*step)

@@ -66,8 +66,8 @@ def merge(queues):
     return text
 
 
-LOADS = [["t1",0,0],["t1",1,0],["c3",1,0],["c3",1,1],["c2",2,0],["c2",0,0],["c2",1,1],["c2",0,1],["c3",0,0],["c2",2,1],["c2",1,0],["c3",0,1],["c2",3,None]]
-LAST = (3, 0)
+LOADS = [["t1",0,0],["t1",1,0],["c2",0,0],["c3",0,0],["c2",0,1],["c3",0,1],["c2",1,1],["c3",1,1],["c2",1,0],["c3",1,0],["c2",2,1],["c2",3,0],["c2",3,1],["c2",2,0]]
+LAST = (3, 1)
 
 
 def parse(text):
@@ -80,9 +80,9 @@ def parse(text):
 
 def queues():
     return {
-        "PE": parse("tr 0, tr 1, tr 2, tr 3, s1 0 0 0, s1 0 0 1, s1 0 0 2, s1 0 0 3, s1 0 1 0, s1 0 1 1, s1 0 1 2, s1 0 1 3, s1 2 0 0, s1 2 0 1, s1 2 0 2, s1 2 0 3, s1 2 1 0, s1 2 1 1, s1 2 1 2, s1 2 1 3, s1 1 0 0, s1 1 0 1, s1 1 0 2, s1 1 0 3, s1 1 1 0, s1 1 1 1, s1 1 1 2, s1 1 1 3, s2 0 2 0, s2 0 2 1, s2 0 2 2, s2 0 2 3, s2 0 3 0, s2 0 3 1, s2 0 3 2, s2 0 3 3, s2 1 3 0, s2 1 3 1, s2 1 3 2, s2 1 3 3, s2 1 2 0, s2 1 2 1, s2 1 2 2, s2 1 2 3, s2 2 3 0, s2 2 3 1, s2 2 3 2, s2 2 3 3, s2 2 2 0, s2 2 2 1, s2 2 2 2, s2 2 2 3, s2 1 0 0, s2 1 0 1, s2 1 0 2, s2 1 0 3, s2 2 0 0, s2 2 0 1, s2 2 0 2, s2 2 0 3, s2 2 1 0, s2 2 1 1, s2 2 1 2, s2 2 1 3, s2 1 1 0, s2 1 1 1, s2 1 1 2, s2 1 1 3, s2 0 0 0, s2 0 0 1, s2 0 0 2, s2 0 0 3, s1 3 0 0, s1 3 0 1, s1 3 0 2, s1 3 0 3, s1 3 1 0, s1 3 1 1, s1 3 1 2, s1 3 1 3, s2 0 1 0, s2 0 1 1, s2 0 1 2, s2 0 1 3, s2 3 3 0, s2 3 3 1, s2 3 3 2, s2 3 3 3, s2 3 2 0, s2 3 2 1, s2 3 2 2, s2 3 2 3, s2 3 0 0, s2 3 0 1, s2 3 0 2, s2 3 0 3, s2 3 1 0, s2 3 1 1, s2 3 1 2, s2 3 1 3"),
-        "S": parse("t1c 0, t1c 1, w 2 0 1, w 2 0 2, w 2 1 0, w 2 1 2, w 2 1 3, w 3 0 1, w 3 0 2, w 3 0 3, w 3 1 0, w 3 1 1, w 3 1 2, w 3 1 3, w 0 0 0, w 0 0 1, w 0 0 2, w 0 0 3, ev1 0 0 0, ev1 0 0 1, ev1 0 0 2, ev1 0 0 3, ev1 0 1 0, ev1 0 1 1, ev1 0 1 2, ev1 0 1 3, ev1 2 0 0, ev1 2 0 1, ev1 2 0 2, ev1 2 0 3, ev1 2 1 0, ev1 2 1 1, ev1 2 1 2, ev1 2 1 3, w 0 1 0, ev1 1 0 0, ev1 1 0 1, ev1 1 0 2, ev1 1 0 3, ev1 1 1 0, ev1 1 1 1, ev1 1 1 2, ev1 1 1 3, ev2 0 2 0, ev2 0 2 1, ev2 0 2 2, ev2 0 2 3, ev2 0 3 0, ev2 0 3 1, ev2 0 3 3, ev2 1 3 1, ev2 1 3 3, ev2 1 2 0, ev2 1 2 1, ev2 1 2 2, ev2 1 2 3, ev2 2 3 0, ev2 2 3 1, ev2 2 3 2, ev2 2 3 3, ev2 2 2 0, ev2 2 2 1, w 1 1 1, w 1 1 2, w 1 1 3, ev2 1 0 1, ev2 1 0 2, ev2 1 0 3, ev2 2 0 0, ev2 2 0 1, ev2 2 0 2, ev2 2 0 3, ev2 2 1 0, ev2 2 1 1, ev2 2 1 2, ev2 2 1 3, ev2 1 1 0, ev2 1 1 1, ev2 1 1 2, ev2 1 1 3, ev2 0 0 0, ev2 0 0 1, ev2 0 0 2, ev2 0 0 3, ev1 3 0 1, ev1 3 0 3, ev1 3 1 1, ev1 3 1 2, ev2 0 1 0, ev2 0 1 1, ev2 0 1 2, ev2 0 1 3, ev2 3 3 0, ev2 3 3 1, ev2 3 3 2, ev2 3 3 3, ev2 3 2 0, ev2 3 2 1, ev2 3 2 2, ev2 3 2 3, ev2 3 0 0, ev2 3 0 1, ev2 3 0 2, ev2 3 0 3, ev2 3 1 0, ev2 3 1 1, ev2 3 1 2, ev2 3 1 3"),
-        "V": parse("w 2 0 0, t1q, w 2 0 3, w 2 1 1, c3i 2 0, w 3 0 0, c3i 2 1, c3q 2 0, c3q 2 1, c2i 0 0, c2i 0 1, c2q 0 0, c2q 0 1, c2i 2 0, c2i 2 1, c2q 2 0, c2q 2 1, t2q 0 0, t2q 0 1, c2i 1 0, c2i 1 1, c2q 1 0, c2q 1 1, c3i 3 0, c3i 3 1, t2q 1 0, c3q 3 0, c3q 3 1, t2q 2 0, t2q 1 1, t2q 2 1, c3i 0 0, ev2 0 3 2, ev2 1 3 0, ev2 1 3 2, w 0 1 1, w 0 1 2, w 0 1 3, w 1 0 0, c3i 0 1, c3q 0 0, c3q 0 1, w 1 0 1, w 1 0 2, w 1 0 3, w 1 1 0, c3i 1 0, ev2 2 2 2, ev2 2 2 3, ev2 1 0 0, c3i 1 1, c3q 1 0, c3q 1 1, c2i 3 0, c2q 3 0, c2i 3 1, c2q 3 1, ev1 3 0 0, ev1 3 0 2, ev1 3 1 0, t2q 3 0, ev1 3 1 3, t2q 3 1"),
+        "PE": parse("tr 0, tr 1, tr 2, tr 3, s1 0 0 1, s1 0 0 0, s1 0 1 1, s1 0 1 3, s1 0 0 2, s1 0 1 2, s1 1 1 3, s1 1 1 0, s1 0 1 0, s1 0 0 3, s1 1 0 1, s1 1 0 3, s1 1 0 2, s1 1 0 0, s1 1 1 1, s1 1 1 2, s2 0 0 2, s2 0 0 0, s2 0 0 1, s2 0 1 0, s2 0 1 2, s2 0 1 1, s2 1 1 3, s2 0 1 3, s2 1 0 3, s2 0 0 3, s2 1 1 2, s2 1 0 0, s2 1 1 1, s1 2 1 0, s1 2 0 1, s1 2 1 1, s1 2 1 2, s1 2 0 0, s2 1 1 0, s2 1 0 2, s1 2 0 3, s2 1 0 1, s1 2 1 3, s1 2 0 2, s2 1 2 3, s2 1 2 0, s2 0 2 2, s2 0 2 3, s2 2 0 1, s2 2 1 1, s2 2 0 0, s2 2 0 2, s2 2 1 2, s2 2 1 0, s2 2 0 3, s2 0 2 1, s2 1 2 1, s2 2 2 0, s2 0 3 3, s2 0 3 1, s2 0 3 2, s2 1 3 3, s2 1 3 1, s2 2 1 3, s1 3 1 2, s1 3 1 1, s1 3 1 0, s2 1 3 2, s1 3 0 1, s1 3 1 3, s2 1 2 2, s2 2 3 0, s1 3 0 2, s2 2 2 3, s1 3 0 0, s2 1 3 0, s1 3 0 3, s2 2 3 1, s2 2 2 1, s2 2 3 3, s2 0 3 0, s2 0 2 0, s2 3 3 2, s2 3 1 3, s2 3 3 3, s2 3 1 2, s2 3 3 0, s2 3 0 2, s2 3 2 3, s2 3 1 0, s2 2 2 2, s2 2 3 2, s2 3 0 1, s2 3 2 1, s2 3 0 3, s2 3 0 0, s2 3 2 0, s2 3 3 1, s2 3 1 1, s2 3 2 2"),
+        "S": parse("t1c 0, t1c 1, w 0 0 1, w 1 0 0, w 1 0 3, w 0 0 2, w 0 0 3, w 1 0 2, w 0 1 3, w 0 1 2, w 1 1 3, ev1 0 0 0, ev1 0 0 1, ev1 0 0 2, w 1 0 1, w 0 1 0, ev1 0 1 1, w 0 1 1, w 1 1 2, ev1 0 1 3, ev1 0 1 0, ev1 1 1 3, ev1 0 1 2, w 2 0 1, ev1 1 0 3, w 2 1 0, ev1 0 0 3, ev1 1 1 1, ev1 1 0 1, ev1 1 1 2, ev1 1 0 2, ev1 1 1 0, ev1 1 0 0, ev2 0 0 1, ev2 0 0 2, w 2 0 3, ev2 0 1 0, ev2 0 1 2, ev2 0 1 1, w 2 1 1, ev2 0 0 0, ev2 0 1 3, ev2 0 0 3, ev2 1 1 3, ev2 1 1 2, ev2 1 0 3, ev1 2 1 0, ev1 2 1 1, ev1 2 0 1, ev2 1 1 0, ev1 2 1 2, ev1 2 0 3, ev1 2 0 0, ev1 2 0 2, ev2 1 0 0, ev2 1 0 2, ev2 1 1 1, ev2 0 2 3, ev2 1 0 1, ev2 2 0 1, ev2 2 1 1, ev2 0 2 2, ev2 2 0 2, ev2 2 1 2, ev2 2 1 0, ev2 2 0 0, ev2 0 2 1, ev2 0 3 3, ev2 0 3 1, ev2 0 3 2, ev2 1 2 1, ev2 1 2 3, ev2 1 3 3, ev2 2 1 3, ev2 1 2 0, ev2 1 3 1, ev2 2 0 3, ev1 3 1 1, ev1 3 1 3, ev2 1 3 2, ev2 1 2 2, ev1 3 0 2, ev1 3 0 1, ev2 1 3 0, ev2 2 3 3, ev2 0 3 0, ev2 0 2 0, ev2 2 2 1, ev2 2 3 1, ev2 3 1 3, ev2 3 3 3, ev2 3 2 3, ev2 3 3 0, ev2 3 1 0, ev2 2 3 2, ev2 2 2 2, ev2 3 0 3, ev2 3 0 0, ev2 3 3 1, ev2 3 1 1, ev2 3 2 2"),
+        "V": parse("c2i 0 0, w 0 0 0, c2q 0 0, t1q, c2i 0 1, c3i 0 0, c2q 0 1, c2i 1 1, c3q 0 0, w 1 1 1, c2q 1 1, c2i 1 0, w 2 0 2, c2q 1 0, c3i 0 1, w 1 1 0, c3q 0 1, c3i 1 1, w 3 1 3, t2q 0 0, t2q 0 1, c3i 1 0, c3q 1 1, c3q 1 0, w 2 1 3, t2q 1 1, t2q 1 0, w 2 0 0, c2i 2 1, c2i 2 0, c2q 2 1, w 2 1 2, c2q 2 0, c3i 2 0, c3i 2 1, c3q 2 0, c3q 2 1, ev1 2 1 3, t2q 2 1, t2q 2 0, w 3 0 1, w 3 1 1, w 3 1 2, w 3 0 3, w 3 0 2, w 3 0 0, w 3 1 0, c3i 3 0, c3i 3 1, c3q 3 0, c3q 3 1, c2i 3 1, c2q 3 1, ev2 2 2 0, c2i 3 0, c2q 3 0, ev1 3 1 2, ev1 3 1 0, ev1 3 0 0, ev2 2 3 0, ev1 3 0 3, t2q 3 0, t2q 3 1, ev2 2 2 3, ev2 3 1 2, ev2 3 0 2, ev2 3 0 1, ev2 3 2 0, ev2 3 3 2, ev2 3 2 1"),
     }
 
 
@@ -91,7 +91,9 @@ def tile_linear2mpo_pa_kernel(tc, t1, core2, core3_bytes, core3_scale, out):
     with ExitStack() as ctx:
         keep = ctx.enter_context(tc.tile_pool(name="keep", bufs=1))
         mid = ctx.enter_context(tc.tile_pool(name="mid", bufs=3))
-        stage = ctx.enter_context(tc.tile_pool(name="stage", bufs=3))
+        mid4 = ctx.enter_context(tc.tile_pool(name="mid4", bufs=4))
+        wide = ctx.enter_context(tc.tile_pool(name="wide", bufs=7))
+        stage = ctx.enter_context(tc.tile_pool(name="stage", bufs=10))
         psum = ctx.enter_context(tc.psum_pool(name="psum", bufs=8))
 
         t1_rows = t1.rearrange("i o k -> (i o) k")
@@ -160,8 +162,8 @@ def tile_linear2mpo_pa_kernel(tc, t1, core2, core3_bytes, core3_scale, out):
                 io, g = a
                 grouped = mid.tile([128, 512, 4], BF16, name="c2_grouped", align_bytes=64)
                 live["c2g", io, g] = grouped
-                copy(e, grouped[:].rearrange("p (t m) j -> p t m j", t=4),
-                     c2_raw[io][:, :, g * 512 : (g + 1) * 512].rearrange("p j (m t) -> p t m j", t=4))
+                copy(e, grouped[:].rearrange("p (t m) j -> p m j t", t=4),
+                     c2_raw[io][:, :, g * 512 : (g + 1) * 512].rearrange("p j (m t) -> p m j t", t=4))
             elif n == "c2q":
                 nc.vector.quantize_mx(out=c2_codes[a][:].bitcast(FP8X4), scales=c2_scales[a][:],
                                       in_=live["c2g", a[0], a[1]][:].rearrange("p n j -> p (n j)"))
@@ -179,7 +181,7 @@ def tile_linear2mpo_pa_kernel(tc, t1, core2, core3_bytes, core3_scale, out):
             elif n == "ev1":
                 io, g, r = a
                 if ("t2g", io, g) not in live:
-                    live["t2g", io, g] = mid.tile([128, 512, 4], BF16, name="t2_grouped", align_bytes=64)
+                    live["t2g", io, g] = mid4.tile([128, 512, 4], BF16, name="t2_grouped", align_bytes=64)
                 copy(e, live["t2g", io, g][:, r * 128 : (r + 1) * 128, :],
                      live["b1", io, g, r][:].rearrange("p (t n) -> p n t", t=4))
             elif n == "t2q":
@@ -188,7 +190,7 @@ def tile_linear2mpo_pa_kernel(tc, t1, core2, core3_bytes, core3_scale, out):
             elif n == "w":
                 c, g, t = a
                 if ("c3w", c, g) not in live:
-                    live["c3w", c, g] = mid.tile([128, 4, 512], BF16, name="c3_wide", align_bytes=64)
+                    live["c3w", c, g] = wide.tile([128, 4, 512], BF16, name="c3_wide", align_bytes=64)
                 src = c3_raw[c // 2, g][:, t, (c % 2) * 512 : (c % 2 + 1) * 512].bitcast(FP8)
                 dst = live["c3w", c, g][:, t, :]
                 if e == "S":
@@ -198,7 +200,7 @@ def tile_linear2mpo_pa_kernel(tc, t1, core2, core3_bytes, core3_scale, out):
             elif n == "c3i":
                 c, g = a
                 live["c3g", c, g] = mid.tile([128, 512, 4], BF16, name="c3_grouped", align_bytes=64)
-                copy(e, live["c3g", c, g][:], live["c3w", c, g][:].rearrange("p t n -> p n t"))
+                copy(e, live["c3g", c, g][:].rearrange("p (n i) t -> p n t i", i=4), live["c3w", c, g][:].rearrange("p t (n i) -> p n t i", i=4))
             elif n == "c3q":
                 nc.vector.quantize_mx(out=c3_codes[a][:].bitcast(FP8X4), scales=c3_scales[a][:],
                                       in_=live["c3g", a[0], a[1]][:].rearrange("p n j -> p (n j)"))
@@ -215,17 +217,15 @@ def tile_linear2mpo_pa_kernel(tc, t1, core2, core3_bytes, core3_scale, out):
             elif n == "ev2":
                 io, c, r = a
                 j = c // 2
-                if ("st", io, j) not in live:
-                    live["st", io, j] = stage.tile([128, 4, 1024], F32, name="result")
-                    live["n", io, j] = []
-                result = live["st", io, j]
-                copy(e, result[:, r, (c % 2) * 512 : (c % 2 + 1) * 512], live["b2", io, c, r][:])
-                live["n", io, j].append(r)
-                group = 2 if (io, j) == LAST else 4
-                r0 = r - r % group
-                if len([x for x in live["n", io, j] if r0 <= x < r0 + group]) == 2 * group:
+                if ("st", io, j, r) not in live:
+                    live["st", io, j, r] = stage.tile([128, 1024], F32, name="result")
+                    live["n", io, j, r] = []
+                result = live["st", io, j, r]
+                copy(e, result[:, (c % 2) * 512 : (c % 2 + 1) * 512], live["b2", io, c, r][:])
+                live["n", io, j, r].append(c)
+                if len(live["n", io, j, r]) == 2:
                     for s in range(4):
-                        nc.sync.dma_start(out=out_v[s, io // 2, j, io % 2][:, r0 : r0 + group, :], in_=result[s:128:4, r0 : r0 + group, :])
+                        nc.sync.dma_start(out=out_v[s, io // 2, j, io % 2][:, r, :], in_=result[s:128:4, :])
 
         with tc.manual_schedule():
             make_identity(nc, ident[:])

from contextlib import ExitStack

import concourse.mybir as mybir
from concourse.masks import make_identity

F32 = mybir.dt.float32
BF16 = mybir.dt.bfloat16
U32 = mybir.dt.uint32
U8 = mybir.dt.uint8
FP8 = mybir.dt.float8_e4m3fn
FP8X4 = mybir.dt.float8_e4m3fn_x4
MULT = mybir.AluOpType.mult
COPY = mybir.ActivationFunctionType.Copy

FLOPS = 2 * 512 * 512 * 4096 + 2 * 2048 * 1024 * 2048


def deps(o):
    n, a = o[0], o[1:]
    if n == "t1c":
        return [("tr", 2 * a[0]), ("tr", 2 * a[0] + 1)]
    if n == "t1q":
        return [("t1c", 0), ("t1c", 1)]
    if n == "c2q":
        return [("c2i",) + a]
    if n == "s1":
        return [("c2q", a[0], a[1]), ("t1q",)]
    if n == "ev1":
        return [("s1",) + a]
    if n == "t2q":
        return [("ev1", a[0], a[1], r) for r in range(4)]
    if n == "c3i":
        return [("w", a[0], a[1], t) for t in range(4)]
    if n == "c3q":
        return [("c3i",) + a]
    if n == "s2":
        return [("t2q", a[0], 0), ("t2q", a[0], 1), ("c3q", a[1], 0), ("c3q", a[1], 1)]
    if n == "ev2":
        return [("s2",) + a]
    return []


def merge(queues):
    pos = {"PE": 0, "S": 0, "V": 0}
    done = set()
    text = []
    live = 0
    while len(text) < len(queues["PE"]) + len(queues["S"]) + len(queues["V"]):
        before = len(text)
        for e in ("PE", "S", "V"):
            while pos[e] < len(queues[e]):
                o = queues[e][pos[e]]
                opens = e == "PE" and not (o[0] == "tr" and o[1] % 2 == 1)
                if opens and live >= 8:
                    break
                if not all(d in done for d in deps(o)):
                    break
                if opens:
                    live += 1
                if o[0] in ("ev1", "ev2", "t1c"):
                    live -= 1
                text.append((e,) + o)
                done.add(o)
                pos[e] += 1
        assert len(text) > before
    return text


LOADS = [["t1",0,0],["t1",1,0],["c2",0,0],["c3",0,0],["c2",0,1],["c3",0,1],["c2",1,1],["c3",1,1],["c2",1,0],["c3",1,0],["c2",2,1],["c2",3,0],["c2",3,1],["c2",2,0]]
LAST = (3, 1)


def parse(text):
    ops = []
    for item in text.split(", "):
        w = item.split(" ")
        ops.append((w[0],) + tuple(int(x) for x in w[1:]))
    return ops


def queues():
    return {
        "PE": parse("tr 0, tr 1, tr 2, tr 3, s1 0 0 1, s1 0 0 0, s1 0 1 1, s1 0 1 3, s1 0 0 2, s1 0 1 2, s1 1 1 3, s1 1 1 0, s1 0 1 0, s1 0 0 3, s1 1 0 1, s1 1 0 3, s1 1 0 2, s1 1 0 0, s1 1 1 1, s1 1 1 2, s2 0 0 2, s2 0 0 0, s2 0 0 1, s2 0 1 0, s2 0 1 2, s2 0 1 1, s2 1 1 3, s2 0 1 3, s2 1 0 3, s2 0 0 3, s2 1 1 2, s2 1 0 0, s2 1 1 1, s1 2 1 0, s1 2 0 1, s1 2 1 1, s1 2 1 2, s1 2 0 0, s2 1 1 0, s2 1 0 2, s1 2 0 3, s2 1 0 1, s1 2 1 3, s1 2 0 2, s2 1 2 3, s2 1 2 0, s2 0 2 2, s2 0 2 3, s2 2 0 1, s2 2 1 1, s2 2 0 0, s2 2 0 2, s2 2 1 2, s2 2 1 0, s2 2 0 3, s2 0 2 1, s2 1 2 1, s2 2 2 0, s2 0 3 3, s2 0 3 1, s2 0 3 2, s2 1 3 3, s2 1 3 1, s2 2 1 3, s1 3 1 2, s1 3 1 1, s1 3 1 0, s2 1 3 2, s1 3 0 1, s1 3 1 3, s2 1 2 2, s2 2 3 0, s1 3 0 2, s2 2 2 3, s1 3 0 0, s2 1 3 0, s1 3 0 3, s2 2 3 1, s2 2 2 1, s2 2 3 3, s2 0 3 0, s2 0 2 0, s2 3 3 2, s2 3 1 3, s2 3 3 3, s2 3 1 2, s2 3 3 0, s2 3 0 2, s2 3 2 3, s2 3 1 0, s2 2 2 2, s2 2 3 2, s2 3 0 1, s2 3 2 1, s2 3 0 3, s2 3 0 0, s2 3 2 0, s2 3 3 1, s2 3 1 1, s2 3 2 2"),
        "S": parse("t1c 0, t1c 1, w 0 0 1, w 1 0 0, w 1 0 3, w 0 0 2, w 0 0 3, w 1 0 2, w 0 1 3, w 0 1 2, w 1 1 3, ev1 0 0 0, ev1 0 0 1, ev1 0 0 2, w 1 0 1, w 0 1 0, ev1 0 1 1, w 0 1 1, w 1 1 2, ev1 0 1 3, ev1 0 1 0, ev1 1 1 3, ev1 0 1 2, w 2 0 1, ev1 1 0 3, w 2 1 0, ev1 0 0 3, ev1 1 1 1, ev1 1 0 1, ev1 1 1 2, ev1 1 0 2, ev1 1 1 0, ev1 1 0 0, ev2 0 0 1, ev2 0 0 2, w 2 0 3, ev2 0 1 0, ev2 0 1 2, ev2 0 1 1, w 2 1 1, ev2 0 0 0, ev2 0 1 3, ev2 0 0 3, ev2 1 1 3, ev2 1 1 2, ev2 1 0 3, ev1 2 1 0, ev1 2 1 1, ev1 2 0 1, ev2 1 1 0, ev1 2 1 2, ev1 2 0 3, ev1 2 0 0, ev1 2 0 2, ev2 1 0 0, ev2 1 0 2, ev2 1 1 1, ev2 0 2 3, ev2 1 0 1, ev2 2 0 1, ev2 2 1 1, ev2 0 2 2, ev2 2 0 2, ev2 2 1 2, ev2 2 1 0, ev2 2 0 0, ev2 0 2 1, ev2 0 3 3, ev2 0 3 1, ev2 0 3 2, ev2 1 2 1, ev2 1 2 3, ev2 1 3 3, ev2 2 1 3, ev2 1 2 0, ev2 1 3 1, ev2 2 0 3, ev1 3 1 1, ev1 3 1 3, ev2 1 3 2, ev2 1 2 2, ev1 3 0 2, ev1 3 0 1, ev2 1 3 0, ev2 2 3 3, ev2 0 3 0, ev2 0 2 0, ev2 2 2 1, ev2 2 3 1, ev2 3 1 3, ev2 3 3 3, ev2 3 2 3, ev2 3 3 0, ev2 3 1 0, ev2 2 3 2, ev2 2 2 2, ev2 3 0 3, ev2 3 0 0, ev2 3 3 1, ev2 3 1 1, ev2 3 2 2"),
        "V": parse("c2i 0 0, w 0 0 0, c2q 0 0, t1q, c2i 0 1, c3i 0 0, c2q 0 1, c2i 1 1, c3q 0 0, w 1 1 1, c2q 1 1, c2i 1 0, w 2 0 2, c2q 1 0, c3i 0 1, w 1 1 0, c3q 0 1, c3i 1 1, w 3 1 3, t2q 0 0, t2q 0 1, c3i 1 0, c3q 1 1, c3q 1 0, w 2 1 3, t2q 1 1, t2q 1 0, w 2 0 0, c2i 2 1, c2i 2 0, c2q 2 1, w 2 1 2, c2q 2 0, c3i 2 0, c3i 2 1, c3q 2 0, c3q 2 1, ev1 2 1 3, t2q 2 1, t2q 2 0, w 3 0 1, w 3 1 1, w 3 1 2, w 3 0 3, w 3 0 2, w 3 0 0, w 3 1 0, c3i 3 0, c3i 3 1, c3q 3 0, c3q 3 1, c2i 3 1, c2q 3 1, ev2 2 2 0, c2i 3 0, c2q 3 0, ev1 3 1 2, ev1 3 1 0, ev1 3 0 0, ev2 2 3 0, ev1 3 0 3, t2q 3 0, t2q 3 1, ev2 2 2 3, ev2 3 1 2, ev2 3 0 2, ev2 3 0 1, ev2 3 2 0, ev2 3 3 2, ev2 3 2 1"),
    }


def tile_linear2mpo_pa_kernel(tc, t1, core2, core3_bytes, core3_scale, out):
    nc = tc.nc
    with ExitStack() as ctx:
        keep = ctx.enter_context(tc.tile_pool(name="keep", bufs=1))
        mid = ctx.enter_context(tc.tile_pool(name="mid", bufs=3))
        mid4 = ctx.enter_context(tc.tile_pool(name="mid4", bufs=4))
        wide = ctx.enter_context(tc.tile_pool(name="wide", bufs=7))
        stage = ctx.enter_context(tc.tile_pool(name="stage", bufs=10))
        psum = ctx.enter_context(tc.psum_pool(name="psum", bufs=8))

        t1_rows = t1.rearrange("i o k -> (i o) k")
        core2_v = core2.rearrange("(p j) i o q -> p j (i o) q", j=4)
        core3_v = core3_bytes.rearrange("(g p t) i o q -> g p t (i o q)", g=2, t=4)
        out_v = out.rearrange("(R s i j) (O o h) q -> s i j o O R (h q)", s=4, i=2, j=2, o=2, h=2)

        ident = keep.tile([128, 128], F32, name="ident")
        perm = keep.tile([128, 128], F32, name="perm")
        scale = keep.tile([128, 2, 4], F32, name="scale")
        t1_raw = keep.tile([128, 4, 512], BF16, name="t1_raw")
        t1_grouped = keep.tile([128, 512, 4], BF16, name="t1_grouped", align_bytes=64)
        t1_codes = keep.tile([128, 512], U32, name="t1_codes", align_bytes=64)
        t1_scales = keep.tile([128, 512], U8, name="t1_scales", align_bytes=64)
        c2_raw = [keep.tile([128, 4, 1024], BF16, name="c2_raw_%d" % io) for io in range(4)]
        c3_raw = {}
        c2_codes, c2_scales, t2_codes, t2_scales, c3_codes, c3_scales = {}, {}, {}, {}, {}, {}
        for a in range(4):
            for g in range(2):
                c2_codes[a, g] = keep.tile([128, 512], U32, name="c2_codes_%d_%d" % (a, g), align_bytes=64)
                c2_scales[a, g] = keep.tile([128, 512], U8, name="c2_scales_%d_%d" % (a, g), align_bytes=64)
                t2_codes[a, g] = keep.tile([128, 512], U32, name="t2_codes_%d_%d" % (a, g), align_bytes=64)
                t2_scales[a, g] = keep.tile([128, 512], U8, name="t2_scales_%d_%d" % (a, g), align_bytes=64)
                c3_codes[a, g] = keep.tile([128, 512], U32, name="c3_codes_%d_%d" % (a, g), align_bytes=64)
                c3_scales[a, g] = keep.tile([128, 512], U8, name="c3_scales_%d_%d" % (a, g), align_bytes=64)
        for h in range(2):
            for g in range(2):
                c3_raw[h, g] = keep.tile([128, 4, 1024], U8, name="c3_raw_%d_%d" % (h, g))

        live = {}

        def copy(e, out_ap, in_ap):
            if e == "S":
                nc.scalar.copy(out_ap, in_ap)
            else:
                nc.vector.tensor_copy(out=out_ap, in_=in_ap)

        def load(kind, a, g):
            if kind == "t1":
                nc.sync.dma_start(out=t1_raw[:, 2 * a : 2 * a + 2, :], in_=t1_rows[a * 256 : (a + 1) * 256, :].rearrange("(r p) k -> p r k", r=2))
            elif kind == "c2" and g is None:
                nc.sync.dma_start(out=c2_raw[a][:], in_=core2_v[:, :, a, :])
            elif kind == "c2":
                cols = slice(g * 512, (g + 1) * 512)
                nc.sync.dma_start(out=c2_raw[a][:, :, cols], in_=core2_v[:, :, a, cols])
            else:
                nc.sync.dma_start(out=c3_raw[a, g][:], in_=core3_v[g][:, :, a * 1024 : (a + 1) * 1024])

        def emit(e, n, *a):
            if n == "tr":
                r = a[0]
                if r % 2 == 0:
                    live["xt", r // 2] = psum.tile([128, 512], F32, name="bank")
                xt = live["xt", r // 2][:].rearrange("p (s u n) -> p s u n", s=2, u=2)
                words = t1_raw[:, r, :].bitcast(F32)
                for u in range(2):
                    nc.tensor.transpose(xt[:, r % 2, u, :], words[:, u::2], perm[:])
            elif n == "t1c":
                dst = t1_grouped[:, a[0] * 256 : (a[0] + 1) * 256, :].rearrange("p n j -> p (n j)").bitcast(F32)
                copy(e, dst.rearrange("p (s n u) -> p s n u", s=2, u=2),
                     live["xt", a[0]][:].rearrange("p (s u n) -> p s n u", s=2, u=2))
            elif n == "t1q":
                nc.vector.quantize_mx(out=t1_codes[:].bitcast(FP8X4), scales=t1_scales[:],
                                      in_=t1_grouped[:].rearrange("p n j -> p (n j)"))
            elif n == "c2i":
                io, g = a
                grouped = mid.tile([128, 512, 4], BF16, name="c2_grouped", align_bytes=64)
                live["c2g", io, g] = grouped
                copy(e, grouped[:].rearrange("p (t m) j -> p m j t", t=4),
                     c2_raw[io][:, :, g * 512 : (g + 1) * 512].rearrange("p j (m t) -> p m j t", t=4))
            elif n == "c2q":
                nc.vector.quantize_mx(out=c2_codes[a][:].bitcast(FP8X4), scales=c2_scales[a][:],
                                      in_=live["c2g", a[0], a[1]][:].rearrange("p n j -> p (n j)"))
            elif n == "s1":
                io, g, r = a
                bank = psum.tile([128, 512], F32, name="bank")
                live["b1", io, g, r] = bank
                rows = slice(r * 128, (r + 1) * 128)
                for t in range(4):
                    cols = slice(t * 128, (t + 1) * 128)
                    nc.tensor.matmul_mx(out=bank[:, cols],
                                        lhsT=c2_codes[io, g][:, cols].bitcast(FP8X4), lhsT_scale=c2_scales[io, g][:, cols],
                                        rhs=t1_codes[:, rows].bitcast(FP8X4), rhs_scale=t1_scales[:, rows],
                                        start=True, stop=True)
            elif n == "ev1":
                io, g, r = a
                if ("t2g", io, g) not in live:
                    live["t2g", io, g] = mid4.tile([128, 512, 4], BF16, name="t2_grouped", align_bytes=64)
                copy(e, live["t2g", io, g][:, r * 128 : (r + 1) * 128, :],
                     live["b1", io, g, r][:].rearrange("p (t n) -> p n t", t=4))
            elif n == "t2q":
                nc.vector.quantize_mx(out=t2_codes[a][:].bitcast(FP8X4), scales=t2_scales[a][:],
                                      in_=live["t2g", a[0], a[1]][:].rearrange("p n j -> p (n j)"))
            elif n == "w":
                c, g, t = a
                if ("c3w", c, g) not in live:
                    live["c3w", c, g] = wide.tile([128, 4, 512], BF16, name="c3_wide", align_bytes=64)
                src = c3_raw[c // 2, g][:, t, (c % 2) * 512 : (c % 2 + 1) * 512].bitcast(FP8)
                dst = live["c3w", c, g][:, t, :]
                if e == "S":
                    nc.scalar.activation(out=dst, in_=src, func=COPY, scale=scale[:, g, t : t + 1])
                else:
                    nc.vector.tensor_scalar(out=dst, in0=src, scalar1=scale[:, g, t : t + 1], scalar2=None, op0=MULT)
            elif n == "c3i":
                c, g = a
                live["c3g", c, g] = mid.tile([128, 512, 4], BF16, name="c3_grouped", align_bytes=64)
                copy(e, live["c3g", c, g][:].rearrange("p (n i) t -> p n t i", i=4), live["c3w", c, g][:].rearrange("p t (n i) -> p n t i", i=4))
            elif n == "c3q":
                nc.vector.quantize_mx(out=c3_codes[a][:].bitcast(FP8X4), scales=c3_scales[a][:],
                                      in_=live["c3g", a[0], a[1]][:].rearrange("p n j -> p (n j)"))
            elif n == "s2":
                io, c, r = a
                bank = psum.tile([128, 512], F32, name="bank")
                live["b2", io, c, r] = bank
                rows = slice(r * 128, (r + 1) * 128)
                for g in range(2):
                    nc.tensor.matmul_mx(out=bank[:],
                                        lhsT=t2_codes[io, g][:, rows].bitcast(FP8X4), lhsT_scale=t2_scales[io, g][:, rows],
                                        rhs=c3_codes[c, g][:].bitcast(FP8X4), rhs_scale=c3_scales[c, g][:],
                                        start=(g == 0), stop=(g == 1))
            elif n == "ev2":
                io, c, r = a
                j = c // 2
                if ("st", io, j, r) not in live:
                    live["st", io, j, r] = stage.tile([128, 1024], F32, name="result")
                    live["n", io, j, r] = []
                result = live["st", io, j, r]
                copy(e, result[:, (c % 2) * 512 : (c % 2 + 1) * 512], live["b2", io, c, r][:])
                live["n", io, j, r].append(c)
                if len(live["n", io, j, r]) == 2:
                    for s in range(4):
                        nc.sync.dma_start(out=out_v[s, io // 2, j, io % 2][:, r, :], in_=result[s:128:4, :])

        with tc.manual_schedule():
            make_identity(nc, ident[:])
            nc.vector.tensor_copy(out=perm[:].rearrange("p (o i) -> p i o", i=4), in_=ident[:].rearrange("p (i o) -> p i o", i=4))
            nc.scalar.dma_start(out=scale[:], in_=core3_scale.rearrange("(g p t) a b c -> p g (t a b c)", g=2, t=4))
            for kind, a, g in LOADS:
                load(kind, a, g)
            for step in merge(queues()):
                emit(*step)
